import numpy as np
import ml_dtypes


def mxq(x, axis, fmt="e4m3"):
    dtype, down = {"e4m3": (ml_dtypes.float8_e4m3fn, 7), "e5m2": (ml_dtypes.float8_e5m2, 14)}[fmt]
    v = np.moveaxis(np.asarray(x, np.float32).astype(ml_dtypes.bfloat16).astype(np.float64), axis, -1)
    blocks = v.reshape(v.shape[:-1] + (-1, 32))
    amax = np.abs(blocks).max(-1, keepdims=True)
    byte = np.maximum(np.where(amax > 0, np.frexp(amax)[1] - 1 + 127, 0) - down, 1)
    scale = np.exp2(byte - 127.0)
    codes = (blocks / scale).astype(np.float32).astype(dtype).astype(np.float64)
    return np.moveaxis((codes * scale).reshape(v.shape), -1, axis)


BF16 = ml_dtypes.bfloat16


def bf(x):
    return np.asarray(x, np.float32).astype(BF16)


def f64(x):
    return np.asarray(x).astype(np.float64)


N, D = 640, 512


def setup_inputs():
    z = np.random.standard_normal((N, D))
    a = np.random.standard_normal((N, 1))
    c = np.random.standard_normal((1, D))
    return {"embeddings": bf((z + a * c) / np.sqrt(D))}


def reference(embeddings):
    e = f64(embeddings)
    sq = np.sum(e * e, axis=-1)
    eq = mxq(e, 1, "e4m3")
    gram = eq @ eq.T
    dist = sq[:, None] + sq[None, :] - 2.0 * gram
    return np.maximum(dist, 0.0)

@@ -1,0 +1,152 @@
+from contextlib import ExitStack
+
+import concourse.mybir as mybir
+from concourse.masks import make_identity
+
+F32 = mybir.dt.float32
+BF16 = mybir.dt.bfloat16
+U32 = mybir.dt.uint32
+U8 = mybir.dt.uint8
+FP8X4 = mybir.dt.float8_e4m3fn_x4
+ALU = mybir.AluOpType
+ACT = mybir.ActivationFunctionType
+
+P = 128
+PACK = 4
+ROWS = 640
+FEATURES = 512
+TILES = ROWS // P
+HALVES = 2
+LEFT = 512
+LEFT_TILES = LEFT // P
+RIGHT = ROWS - LEFT
+PSUM_BANKS = 8
+
+FLOPS = 2 * ROWS * ROWS * FEATURES
+
+
+def tile_rdm_module_s_kernel(tc, embeddings, out):
+    nc = tc.nc
+    with ExitStack() as ctx:
+        keep = ctx.enter_context(tc.tile_pool(name="keep", bufs=1))
+        work = ctx.enter_context(tc.tile_pool(name="work", bufs=TILES))
+        psum_sq = ctx.enter_context(tc.psum_pool(name="psum_sq", bufs=1))
+        psum = ctx.enter_context(tc.psum_pool(name="psum", bufs=PSUM_BANKS - 2))
+        ctx.enter_context(tc.manual_schedule())
+
+        x = keep.tile([P, TILES, FEATURES], BF16)
+        squares = keep.tile([P, TILES, FEATURES], BF16)
+        sq_col = keep.tile([P, TILES], F32)
+        sq_row = keep.tile([P, ROWS], F32)
+        ident = keep.tile([P, P], F32)
+        grouped = keep.tile([P, ROWS * PACK], BF16, align_bytes=64)
+        codes = keep.tile([P, ROWS], U32, align_bytes=64)
+        scales = keep.tile([P, ROWS], U8, align_bytes=64)
+        grouped_words = grouped[:].bitcast(F32).rearrange("p (i h) -> p i h", h=HALVES)
+        right_partial = keep.tile([P, TILES, RIGHT], F32)
+        right_dist = keep.tile([P, TILES, RIGHT], F32)
+        out_right = out.rearrange("(m p) j -> p m j", p=P)[:, :, LEFT:]
+
+        def tile_cols(t):
+            return slice(t * P, (t + 1) * P)
+
+        def flip(t):
+            words = x[:, t, :].bitcast(F32).rearrange("p (w h) -> p h w", h=HALVES)
+            flipped = psum.tile([P, HALVES, P], F32, tag="bank")
+            for h in range(HALVES):
+                nc.tensor.transpose(flipped[:, h, :], words[:, h, :], ident[:])
+            nc.vector.tensor_copy(
+                out=grouped_words[:, tile_cols(t), :],
+                in_=flipped[:].rearrange("p h i -> p i h"),
+            )
+
+        def quantise(t):
+            nc.vector.quantize_mx(
+                out=codes[:, tile_cols(t)].bitcast(FP8X4),
+                scales=scales[:, tile_cols(t)],
+                in_=grouped[:, t * P * PACK : (t + 1) * P * PACK],
+            )
+
+        def spread(t, target):
+            nc.tensor.transpose(target, sq_col[:, t : t + 1].to_broadcast([P, P]), ident[:])
+
+        def gram_block(target, m, cols):
+            nc.tensor.matmul_mx(
+                out=target,
+                lhsT=codes[:, tile_cols(m)].bitcast(FP8X4),
+                lhsT_scale=scales[:, tile_cols(m)],
+                rhs=codes[:, cols].bitcast(FP8X4),
+                rhs_scale=scales[:, cols],
+                start=True,
+                stop=True,
+            )
+
+        def left(m):
+            gram = psum.tile([P, LEFT], F32, tag="bank")
+            gram_block(gram[:], m, slice(0, LEFT))
+            partial = work.tile([P, LEFT], F32)
+            nc.vector.scalar_tensor_tensor(
+                out=partial[:],
+                in0=gram[:],
+                scalar=-2.0,
+                in1=sq_row[:, :LEFT],
+                op0=ALU.mult,
+                op1=ALU.add,
+            )
+            dist = work.tile([P, LEFT], F32)
+            nc.scalar.activation(
+                out=dist[:], in_=partial[:], func=ACT.Relu, bias=sq_col[:, m : m + 1], scale=1.0
+            )
+            nc.sync.dma_start(out=out[tile_cols(m), :LEFT], in_=dist[:])
+
+        def right_first_step(first, count):
+            gram = psum.tile([P, count, RIGHT], F32, tag="bank")
+            for b in range(count):
+                gram_block(gram[:, b, :], first + b, slice(LEFT, ROWS))
+            nc.vector.scalar_tensor_tensor(
+                out=right_partial[:, first : first + count, :],
+                in0=gram[:],
+                scalar=-2.0,
+                in1=sq_row[:, LEFT:].unsqueeze(1).to_broadcast([P, count, RIGHT]),
+                op0=ALU.mult,
+                op1=ALU.add,
+            )
+
+        for t in range(TILES):
+            nc.sync.dma_start(out=x[:, t, :], in_=embeddings[tile_cols(t), :])
+        make_identity(nc, ident[:])
+
+        for t in range(TILES):
+            nc.scalar.activation(
+                out=squares[:, t, :],
+                in_=x[:, t, :],
+                func=ACT.Square,
+                accum_out=sq_col[:, t : t + 1],
+            )
+            flip(t)
+            if t > 0:
+                quantise(t - 1)
+        quantise(TILES - 1)
+
+        spread_left = psum_sq.tile([P, LEFT], F32)
+        for t in range(LEFT_TILES):
+            spread(t, spread_left[:, tile_cols(t)])
+        nc.vector.tensor_copy(out=sq_row[:, :LEFT], in_=spread_left[:])
+        for m in range(TILES):
+            left(m)
+
+        spread_right = psum_sq.tile([P, RIGHT], F32)
+        spread(LEFT_TILES, spread_right[:])
+        nc.vector.tensor_copy(out=sq_row[:, LEFT:], in_=spread_right[:])
+        right_first_step(0, LEFT_TILES)
+        right_first_step(LEFT_TILES, TILES - LEFT_TILES)
+        for m in range(TILES):
+            nc.vector.tensor_scalar(
+                out=right_dist[:, m, :],
+                in0=right_partial[:, m, :],
+                scalar1=sq_col[:, m : m + 1],
+                scalar2=0.0,
+                op0=ALU.add,
+                op1=ALU.max,
+            )
+        nc.sync.dma_start(out=out_right, in_=right_dist[:])

@@ -36,7 +36,8 @@ def tile_rdm_module_s_kernel(tc, embeddings, out):
 
         x = keep.tile([P, TILES, FEATURES], BF16)
         squares = keep.tile([P, TILES, FEATURES], BF16)
-        sq_col = keep.tile([P, TILES], F32)
+        sq_col_v = keep.tile([P, 1], F32)
+        sq_col_s = keep.tile([P, TILES], F32)
         sq_row = keep.tile([P, ROWS], F32)
         ident = keep.tile([P, P], F32)
         grouped = keep.tile([P, ROWS * PACK], BF16, align_bytes=64)
@@ -49,6 +50,28 @@ def tile_rdm_module_s_kernel(tc, embeddings, out):
 
         def tile_cols(t):
             return slice(t * P, (t + 1) * P)
+
+        def square_sum(t):
+            if t == 0:
+                nc.vector.scalar_tensor_tensor(
+                    out=squares[:, t, :],
+                    in0=x[:, t, :],
+                    scalar=1.0,
+                    in1=x[:, t, :],
+                    op0=ALU.mult,
+                    op1=ALU.mult,
+                    accum_out=sq_col_v[:],
+                )
+            else:
+                nc.scalar.activation(
+                    out=squares[:, t, :],
+                    in_=x[:, t, :],
+                    func=ACT.Square,
+                    accum_out=sq_col_s[:, t : t + 1],
+                )
+
+        def sq_of(t):
+            return sq_col_v[:] if t == 0 else sq_col_s[:, t : t + 1]
 
         def flip(t):
             words = x[:, t, :].bitcast(F32).rearrange("p (w h) -> p h w", h=HALVES)
@@ -68,7 +91,7 @@ def tile_rdm_module_s_kernel(tc, embeddings, out):
             )
 
         def spread(t, target):
-            nc.tensor.transpose(target, sq_col[:, t : t + 1].to_broadcast([P, P]), ident[:])
+            nc.tensor.transpose(target, sq_of(t).to_broadcast([P, P]), ident[:])
 
         def gram_block(target, m, cols):
             nc.tensor.matmul_mx(
@@ -95,7 +118,7 @@ def tile_rdm_module_s_kernel(tc, embeddings, out):
             )
             dist = work.tile([P, LEFT], F32)
             nc.scalar.activation(
-                out=dist[:], in_=partial[:], func=ACT.Relu, bias=sq_col[:, m : m + 1], scale=1.0
+                out=dist[:], in_=partial[:], func=ACT.Relu, bias=sq_of(m), scale=1.0
             )
             nc.sync.dma_start(out=out[tile_cols(m), :LEFT], in_=dist[:])
 
@@ -117,12 +140,7 @@ def tile_rdm_module_s_kernel(tc, embeddings, out):
         make_identity(nc, ident[:])
 
         for t in range(TILES):
-            nc.scalar.activation(
-                out=squares[:, t, :],
-                in_=x[:, t, :],
-                func=ACT.Square,
-                accum_out=sq_col[:, t : t + 1],
-            )
+            square_sum(t)
             flip(t)
             if t > 0:
                 quantise(t - 1)
@@ -131,20 +149,20 @@ def tile_rdm_module_s_kernel(tc, embeddings, out):
         spread_left = psum_sq.tile([P, LEFT], F32)
         for t in range(LEFT_TILES):
             spread(t, spread_left[:, tile_cols(t)])
-        nc.vector.tensor_copy(out=sq_row[:, :LEFT], in_=spread_left[:])
+        nc.scalar.copy(out=sq_row[:, :LEFT], in_=spread_left[:])
+        spread_right = psum_sq.tile([P, RIGHT], F32)
+        spread(LEFT_TILES, spread_right[:])
+        nc.scalar.copy(out=sq_row[:, LEFT:], in_=spread_right[:])
         for m in range(TILES):
             left(m)
 
-        spread_right = psum_sq.tile([P, RIGHT], F32)
-        spread(LEFT_TILES, spread_right[:])
-        nc.vector.tensor_copy(out=sq_row[:, LEFT:], in_=spread_right[:])
         right_first_step(0, LEFT_TILES)
         right_first_step(LEFT_TILES, TILES - LEFT_TILES)
         for m in range(TILES):
             nc.vector.tensor_scalar(
                 out=right_dist[:, m, :],
                 in0=right_partial[:, m, :],
-                scalar1=sq_col[:, m : m + 1],
+                scalar1=sq_of(m),
                 scalar2=0.0,
                 op0=ALU.add,
                 op1=ALU.max,

@@ -29,9 +29,8 @@ def tile_rdm_module_s_kernel(tc, embeddings, out):
     nc = tc.nc
     with ExitStack() as ctx:
         keep = ctx.enter_context(tc.tile_pool(name="keep", bufs=1))
-        work = ctx.enter_context(tc.tile_pool(name="work", bufs=TILES))
         psum_sq = ctx.enter_context(tc.psum_pool(name="psum_sq", bufs=1))
-        psum = ctx.enter_context(tc.psum_pool(name="psum", bufs=PSUM_BANKS - 2))
+        psum = ctx.enter_context(tc.psum_pool(name="psum", bufs=PSUM_BANKS - 3))
         ctx.enter_context(tc.manual_schedule())
 
         x = keep.tile([P, TILES, FEATURES], BF16)
@@ -44,12 +43,12 @@ def tile_rdm_module_s_kernel(tc, embeddings, out):
         codes = keep.tile([P, ROWS], U32, align_bytes=64)
         scales = keep.tile([P, ROWS], U8, align_bytes=64)
         grouped_words = grouped[:].bitcast(F32).rearrange("p (i h) -> p i h", h=HALVES)
-        right_partial = keep.tile([P, TILES, RIGHT], F32)
-        right_dist = keep.tile([P, TILES, RIGHT], F32)
-        out_right = out.rearrange("(m p) j -> p m j", p=P)[:, :, LEFT:]
+        partial = keep.tile([P, TILES, ROWS], F32)
+        dist = keep.tile([P, TILES, ROWS], F32)
+        out_tiles = out.rearrange("(m p) j -> p m j", p=P)
 
-        def tile_cols(t):
-            return slice(t * P, (t + 1) * P)
+        def tile_cols(first, count=1):
+            return slice(first * P, (first + count) * P)
 
         def square_sum(t):
             if t == 0:
@@ -73,14 +72,19 @@ def tile_rdm_module_s_kernel(tc, embeddings, out):
         def sq_of(t):
             return sq_col_v[:] if t == 0 else sq_col_s[:, t : t + 1]
 
+        flipped = {}
+
         def flip(t):
             words = x[:, t, :].bitcast(F32).rearrange("p (w h) -> p h w", h=HALVES)
-            flipped = psum.tile([P, HALVES, P], F32, tag="bank")
+            bank = psum.tile([P, HALVES, P], F32, tag="bank")
             for h in range(HALVES):
-                nc.tensor.transpose(flipped[:, h, :], words[:, h, :], ident[:])
+                nc.tensor.transpose(bank[:, h, :], words[:, h, :], ident[:])
+            flipped[t] = bank
+
+        def regroup(t):
             nc.vector.tensor_copy(
                 out=grouped_words[:, tile_cols(t), :],
-                in_=flipped[:].rearrange("p h i -> p i h"),
+                in_=flipped[t][:].rearrange("p h i -> p i h"),
             )
 
         def quantise(t):
@@ -90,81 +94,120 @@ def tile_rdm_module_s_kernel(tc, embeddings, out):
                 in_=grouped[:, t * P * PACK : (t + 1) * P * PACK],
             )
 
-        def spread(t, target):
-            nc.tensor.transpose(target, sq_of(t).to_broadcast([P, P]), ident[:])
-
-        def gram_block(target, m, cols):
-            nc.tensor.matmul_mx(
-                out=target,
-                lhsT=codes[:, tile_cols(m)].bitcast(FP8X4),
-                lhsT_scale=scales[:, tile_cols(m)],
-                rhs=codes[:, cols].bitcast(FP8X4),
-                rhs_scale=scales[:, cols],
-                start=True,
-                stop=True,
-            )
-
-        def left(m):
-            gram = psum.tile([P, LEFT], F32, tag="bank")
-            gram_block(gram[:], m, slice(0, LEFT))
-            partial = work.tile([P, LEFT], F32)
-            nc.vector.scalar_tensor_tensor(
-                out=partial[:],
-                in0=gram[:],
-                scalar=-2.0,
-                in1=sq_row[:, :LEFT],
-                op0=ALU.mult,
-                op1=ALU.add,
-            )
-            dist = work.tile([P, LEFT], F32)
-            nc.scalar.activation(
-                out=dist[:], in_=partial[:], func=ACT.Relu, bias=sq_of(m), scale=1.0
-            )
-            nc.sync.dma_start(out=out[tile_cols(m), :LEFT], in_=dist[:])
-
-        def right_first_step(first, count):
-            gram = psum.tile([P, count, RIGHT], F32, tag="bank")
+        def spread(first, count):
+            bank = psum_sq.tile([P, count * P], F32, tag="sq%d" % first)
             for b in range(count):
-                gram_block(gram[:, b, :], first + b, slice(LEFT, ROWS))
+                nc.tensor.transpose(
+                    bank[:, tile_cols(b)], sq_of(first + b).to_broadcast([P, P]), ident[:]
+                )
+            return bank
+
+        def keep_sq(first, count, bank):
+            nc.scalar.copy(out=sq_row[:, tile_cols(first, count)], in_=bank[:])
+
+        def gram(m, rows, c, cols):
+            bank = psum.tile([P, rows, cols * P], F32, tag="bank")
+            for b in range(rows):
+                nc.tensor.matmul_mx(
+                    out=bank[:, b, :],
+                    lhsT=codes[:, tile_cols(m + b)].bitcast(FP8X4),
+                    lhsT_scale=scales[:, tile_cols(m + b)],
+                    rhs=codes[:, tile_cols(c, cols)].bitcast(FP8X4),
+                    rhs_scale=scales[:, tile_cols(c, cols)],
+                    start=True,
+                    stop=True,
+                )
+            return bank
+
+        def first_step(m, rows, c, cols, bank):
             nc.vector.scalar_tensor_tensor(
-                out=right_partial[:, first : first + count, :],
-                in0=gram[:],
+                out=partial[:, m : m + rows, tile_cols(c, cols)],
+                in0=bank[:],
                 scalar=-2.0,
-                in1=sq_row[:, LEFT:].unsqueeze(1).to_broadcast([P, count, RIGHT]),
+                in1=sq_row[:, tile_cols(c, cols)].unsqueeze(1).to_broadcast([P, rows, cols * P]),
                 op0=ALU.mult,
                 op1=ALU.add,
+            )
+
+        def second_step(m, c, cols):
+            nc.scalar.activation(
+                out=dist[:, m, tile_cols(c, cols)],
+                in_=partial[:, m, tile_cols(c, cols)],
+                func=ACT.Relu,
+                bias=sq_of(m),
+                scale=1.0,
+            )
+
+        def second_step_vector(m, c, cols):
+            nc.vector.tensor_scalar(
+                out=dist[:, m, tile_cols(c, cols)],
+                in0=partial[:, m, tile_cols(c, cols)],
+                scalar1=sq_of(m),
+                scalar2=0.0,
+                op0=ALU.add,
+                op1=ALU.max,
+            )
+
+        def store(m, rows, c, cols):
+            nc.sync.dma_start(
+                out=out_tiles[:, m : m + rows, tile_cols(c, cols)],
+                in_=dist[:, m : m + rows, tile_cols(c, cols)],
             )
 
         for t in range(TILES):
             nc.sync.dma_start(out=x[:, t, :], in_=embeddings[tile_cols(t), :])
         make_identity(nc, ident[:])
 
-        for t in range(TILES):
+        for t in range(3):
             square_sum(t)
             flip(t)
-            if t > 0:
-                quantise(t - 1)
-        quantise(TILES - 1)
-
-        spread_left = psum_sq.tile([P, LEFT], F32)
-        for t in range(LEFT_TILES):
-            spread(t, spread_left[:, tile_cols(t)])
-        nc.scalar.copy(out=sq_row[:, :LEFT], in_=spread_left[:])
-        spread_right = psum_sq.tile([P, RIGHT], F32)
-        spread(LEFT_TILES, spread_right[:])
-        nc.scalar.copy(out=sq_row[:, LEFT:], in_=spread_right[:])
-        for m in range(TILES):
-            left(m)
-
-        right_first_step(0, LEFT_TILES)
-        right_first_step(LEFT_TILES, TILES - LEFT_TILES)
-        for m in range(TILES):
-            nc.vector.tensor_scalar(
-                out=right_dist[:, m, :],
-                in0=right_partial[:, m, :],
-                scalar1=sq_of(m),
-                scalar2=0.0,
-                op0=ALU.add,
-                op1=ALU.max,
-            )
-        nc.sync.dma_start(out=out_right, in_=right_dist[:])
+        sq_bank0 = spread(0, 2)
+        flip(3)
+        flip(4)
+        regroup(0)
+        regroup(1)
+        quantise(0)
+        regroup(2)
+        quantise(1)
+        keep_sq(0, 2, sq_bank0)
+        square_sum(3)
+        gram_a = gram(0, 2, 0, 2)
+        regroup(3)
+        quantise(2)
+        regroup(4)
+        quantise(3)
+        sq_bank2 = spread(2, 2)
+        first_step(0, 2, 0, 2, gram_a)
+        quantise(4)
+        square_sum(4)
+        keep_sq(2, 2, sq_bank2)
+        gram_b = gram(0, 2, 2, 2)
+        sq_bank4 = spread(4, 1)
+        for m in range(2):
+            second_step(m, 0, 2)
+            store(m, 1, 0, 2)
+        first_step(0, 2, 2, 2, gram_b)
+        keep_sq(4, 1, sq_bank4)
+        for m in range(2):
+            second_step(m, 2, 2)
+            store(m, 1, 2, 2)
+        gram_c = gram(2, 1, 0, 4)
+        first_step(2, 1, 0, 4, gram_c)
+        second_step(2, 0, 4)
+        store(2, 1, 0, 4)
+        gram_d = gram(3, 1, 0, 4)
+        gram_r = gram(0, 4, 4, 1)
+        first_step(0, 4, 4, 1, gram_r)
+        gram_f = gram(4, 1, 0, 4)
+        first_step(4, 1, 0, 4, gram_f)
+        gram_g = gram(4, 1, 4, 1)
+        first_step(4, 1, 4, 1, gram_g)
+        for m in range(4):
+            second_step(m, 4, 1)
+        store(0, 4, 4, 1)
+        first_step(3, 1, 0, 4, gram_d)
+        second_step(4, 0, 4)
+        second_step_vector(4, 4, 1)
+        store(4, 1, 0, 5)
+        second_step_vector(3, 0, 4)
+        store(3, 1, 0, 4)

@@ -21,6 +21,7 @@ LEFT = 512
 LEFT_TILES = LEFT // P
 RIGHT = ROWS - LEFT
 PSUM_BANKS = 8
+WARM_UP = 3
 
 FLOPS = 2 * ROWS * ROWS * FEATURES
 
@@ -156,6 +157,11 @@ def tile_rdm_module_s_kernel(tc, embeddings, out):
 
         for t in range(TILES):
             nc.sync.dma_start(out=x[:, t, :], in_=embeddings[tile_cols(t), :])
+        zeros = keep.tile([P, P], F32)
+        nc.vector.memset(zeros[:], 0.0)
+        idle_bank = psum.tile([P, P], F32, tag="bank")
+        for w in range(WARM_UP):
+            nc.tensor.matmul(idle_bank[:], lhsT=zeros[:], rhs=zeros[:], start=True, stop=True)
         make_identity(nc, ident[:])
 
         for t in range(3):

@@ -21,7 +21,6 @@ LEFT = 512
 LEFT_TILES = LEFT // P
 RIGHT = ROWS - LEFT
 PSUM_BANKS = 8
-WARM_UP = 3
 
 FLOPS = 2 * ROWS * ROWS * FEATURES
 
@@ -159,17 +158,25 @@ def tile_rdm_module_s_kernel(tc, embeddings, out):
             nc.sync.dma_start(out=x[:, t, :], in_=embeddings[tile_cols(t), :])
         zeros = keep.tile([P, P], F32)
         nc.vector.memset(zeros[:], 0.0)
-        idle_bank = psum.tile([P, P], F32, tag="bank")
-        for w in range(WARM_UP):
-            nc.tensor.matmul(idle_bank[:], lhsT=zeros[:], rhs=zeros[:], start=True, stop=True)
+        idle_bank = psum_sq.tile([P, P], F32, tag="idle")
+
+        def keep_busy(count):
+            for w in range(count):
+                nc.tensor.matmul(idle_bank[:], lhsT=zeros[:], rhs=zeros[:], start=True, stop=True)
+
+        keep_busy(3)
         make_identity(nc, ident[:])
 
         for t in range(3):
             square_sum(t)
-            flip(t)
-        sq_bank0 = spread(0, 2)
+        flip(0)
+        flip(1)
+        keep_busy(1)
+        flip(2)
         flip(3)
+        sq_bank0 = spread(0, 2)
         flip(4)
+        keep_busy(1)
         regroup(0)
         regroup(1)
         quantise(0)
@@ -177,43 +184,47 @@ def tile_rdm_module_s_kernel(tc, embeddings, out):
         quantise(1)
         keep_sq(0, 2, sq_bank0)
         square_sum(3)
-        gram_a = gram(0, 2, 0, 2)
+        square_sum(4)
         regroup(3)
         quantise(2)
-        regroup(4)
         quantise(3)
-        sq_bank2 = spread(2, 2)
+        gram_a = gram(0, 2, 0, 2)
         first_step(0, 2, 0, 2, gram_a)
+        regroup(4)
+        gram_b = gram(2, 2, 0, 2)
+        sq_bank2 = spread(2, 3)
+        second_step(0, 0, 2)
+        store(0, 1, 0, 2)
+        keep_sq(2, 3, sq_bank2)
+        first_step(2, 2, 0, 2, gram_b)
         quantise(4)
-        square_sum(4)
-        keep_sq(2, 2, sq_bank2)
-        gram_b = gram(0, 2, 2, 2)
-        sq_bank4 = spread(4, 1)
-        for m in range(2):
+        second_step(1, 0, 2)
+        store(1, 1, 0, 2)
+        gram_c = gram(0, 2, 2, 2)
+        gram_d = gram(2, 2, 2, 2)
+        gram_f = gram(4, 1, 0, 4)
+        gram_r = gram(0, 4, 4, 1)
+        gram_g = gram(4, 1, 4, 1)
+        first_step(0, 2, 2, 2, gram_c)
+        for m in (2, 3):
             second_step(m, 0, 2)
             store(m, 1, 0, 2)
-        first_step(0, 2, 2, 2, gram_b)
-        keep_sq(4, 1, sq_bank4)
-        for m in range(2):
+        first_step(2, 2, 2, 2, gram_d)
+        for m in (0, 1):
             second_step(m, 2, 2)
             store(m, 1, 2, 2)
-        gram_c = gram(2, 1, 0, 4)
-        first_step(2, 1, 0, 4, gram_c)
-        second_step(2, 0, 4)
-        store(2, 1, 0, 4)
-        gram_d = gram(3, 1, 0, 4)
-        gram_r = gram(0, 4, 4, 1)
-        first_step(0, 4, 4, 1, gram_r)
-        gram_f = gram(4, 1, 0, 4)
         first_step(4, 1, 0, 4, gram_f)
-        gram_g = gram(4, 1, 4, 1)
+        for m in (2, 3):
+            second_step(m, 2, 2)
+            store(m, 1, 2, 2)
         first_step(4, 1, 4, 1, gram_g)
-        for m in range(4):
-            second_step(m, 4, 1)
-        store(0, 4, 4, 1)
-        first_step(3, 1, 0, 4, gram_d)
+        first_step(0, 4, 4, 1, gram_r)
         second_step(4, 0, 4)
         second_step_vector(4, 4, 1)
         store(4, 1, 0, 5)
-        second_step_vector(3, 0, 4)
-        store(3, 1, 0, 4)
+        for m in (0, 1):
+            second_step_vector(m, 4, 1)
+        store(0, 2, 4, 1)
+        for m in (2, 3):
+            second_step(m, 4, 1)
+        store(2, 2, 4, 1)

@@ -81,8 +81,9 @@ def tile_rdm_module_s_kernel(tc, embeddings, out):
                 nc.tensor.transpose(bank[:, h, :], words[:, h, :], ident[:])
             flipped[t] = bank
 
-        def regroup(t):
-            nc.vector.tensor_copy(
+        def regroup(t, on_scalar=False):
+            copy = nc.scalar.copy if on_scalar else nc.vector.tensor_copy
+            copy(
                 out=grouped_words[:, tile_cols(t), :],
                 in_=flipped[t][:].rearrange("p h i -> p i h"),
             )
@@ -158,7 +159,7 @@ def tile_rdm_module_s_kernel(tc, embeddings, out):
             nc.sync.dma_start(out=x[:, t, :], in_=embeddings[tile_cols(t), :])
         zeros = keep.tile([P, P], F32)
         nc.vector.memset(zeros[:], 0.0)
-        idle_bank = psum_sq.tile([P, P], F32, tag="idle")
+        idle_bank = psum_sq.tile([P, P], F32, tag="sq4")
 
         def keep_busy(count):
             for w in range(count):
@@ -167,15 +168,11 @@ def tile_rdm_module_s_kernel(tc, embeddings, out):
         keep_busy(3)
         make_identity(nc, ident[:])
 
-        for t in range(3):
+        for t in range(4):
             square_sum(t)
-        flip(0)
-        flip(1)
-        keep_busy(1)
-        flip(2)
-        flip(3)
+        for t in range(TILES):
+            flip(t)
         sq_bank0 = spread(0, 2)
-        flip(4)
         keep_busy(1)
         regroup(0)
         regroup(1)
@@ -183,22 +180,23 @@ def tile_rdm_module_s_kernel(tc, embeddings, out):
         regroup(2)
         quantise(1)
         keep_sq(0, 2, sq_bank0)
-        square_sum(3)
         square_sum(4)
+        gram_a = gram(0, 2, 0, 2)
         regroup(3)
         quantise(2)
         quantise(3)
-        gram_a = gram(0, 2, 0, 2)
         first_step(0, 2, 0, 2, gram_a)
-        regroup(4)
+        regroup(4, on_scalar=True)
         gram_b = gram(2, 2, 0, 2)
-        sq_bank2 = spread(2, 3)
+        keep_busy(1)
+        sq_bank2 = spread(2, 2)
+        sq_bank4 = spread(4, 1)
         second_step(0, 0, 2)
         store(0, 1, 0, 2)
-        keep_sq(2, 3, sq_bank2)
+        keep_sq(2, 2, sq_bank2)
         first_step(2, 2, 0, 2, gram_b)
         quantise(4)
-        second_step(1, 0, 2)
+        second_step_vector(1, 0, 2)
         store(1, 1, 0, 2)
         gram_c = gram(0, 2, 2, 2)
         gram_d = gram(2, 2, 2, 2)
@@ -209,22 +207,23 @@ def tile_rdm_module_s_kernel(tc, embeddings, out):
         for m in (2, 3):
             second_step(m, 0, 2)
             store(m, 1, 0, 2)
-        first_step(2, 2, 2, 2, gram_d)
+        keep_sq(4, 1, sq_bank4)
+        first_step(4, 1, 0, 4, gram_f)
         for m in (0, 1):
             second_step(m, 2, 2)
             store(m, 1, 2, 2)
-        first_step(4, 1, 0, 4, gram_f)
+        first_step(2, 2, 2, 2, gram_d)
+        second_step(4, 0, 4)
+        store(4, 1, 0, 4)
+        first_step(4, 1, 4, 1, gram_g)
+        first_step(0, 4, 4, 1, gram_r)
         for m in (2, 3):
             second_step(m, 2, 2)
             store(m, 1, 2, 2)
-        first_step(4, 1, 4, 1, gram_g)
-        first_step(0, 4, 4, 1, gram_r)
-        second_step(4, 0, 4)
         second_step_vector(4, 4, 1)
-        store(4, 1, 0, 5)
         for m in (0, 1):
             second_step_vector(m, 4, 1)
         store(0, 2, 4, 1)
-        for m in (2, 3):
-            second_step(m, 4, 1)
-        store(2, 2, 4, 1)
+        second_step(2, 4, 1)
+        second_step_vector(3, 4, 1)
+        store(2, 3, 4, 1)

@@ -75,7 +75,7 @@ def tile_rdm_module_s_kernel(tc, embeddings, out):
         flipped = {}
 
         def flip(t):
-            words = x[:, t, :].bitcast(F32).rearrange("p (w h) -> p h w", h=HALVES)
+            words = x[:, t, :].bitcast(F32).rearrange("p (h w) -> p h w", h=HALVES)
             bank = psum.tile([P, HALVES, P], F32, tag="bank")
             for h in range(HALVES):
                 nc.tensor.transpose(bank[:, h, :], words[:, h, :], ident[:])
@@ -161,19 +161,24 @@ def tile_rdm_module_s_kernel(tc, embeddings, out):
         nc.vector.memset(zeros[:], 0.0)
         idle_bank = psum_sq.tile([P, P], F32, tag="sq4")
 
-        def keep_busy(count):
+        def keep_busy(count, cols=P):
             for w in range(count):
-                nc.tensor.matmul(idle_bank[:], lhsT=zeros[:], rhs=zeros[:], start=True, stop=True)
+                nc.tensor.matmul(
+                    idle_bank[:, :cols], lhsT=zeros[:], rhs=zeros[:, :cols], start=True, stop=True
+                )
 
         keep_busy(3)
         make_identity(nc, ident[:])
 
         for t in range(4):
             square_sum(t)
-        for t in range(TILES):
+        flip(0)
+        flip(1)
+        keep_busy(1)
+        for t in range(2, TILES):
             flip(t)
         sq_bank0 = spread(0, 2)
-        keep_busy(1)
+        keep_busy(1, P // 2)
         regroup(0)
         regroup(1)
         quantise(0)
@@ -188,7 +193,6 @@ def tile_rdm_module_s_kernel(tc, embeddings, out):
         first_step(0, 2, 0, 2, gram_a)
         regroup(4, on_scalar=True)
         gram_b = gram(2, 2, 0, 2)
-        keep_busy(1)
         sq_bank2 = spread(2, 2)
         sq_bank4 = spread(4, 1)
         second_step(0, 0, 2)

@@ -203,31 +203,29 @@ def tile_rdm_module_s_kernel(tc, embeddings, out):
         second_step_vector(1, 0, 2)
         store(1, 1, 0, 2)
         gram_c = gram(0, 2, 2, 2)
+        gram_r = gram(0, 4, 4, 1)
         gram_d = gram(2, 2, 2, 2)
         gram_f = gram(4, 1, 0, 4)
-        gram_r = gram(0, 4, 4, 1)
         gram_g = gram(4, 1, 4, 1)
         first_step(0, 2, 2, 2, gram_c)
         for m in (2, 3):
             second_step(m, 0, 2)
             store(m, 1, 0, 2)
         keep_sq(4, 1, sq_bank4)
-        first_step(4, 1, 0, 4, gram_f)
+        first_step(0, 4, 4, 1, gram_r)
         for m in (0, 1):
             second_step(m, 2, 2)
             store(m, 1, 2, 2)
         first_step(2, 2, 2, 2, gram_d)
-        second_step(4, 0, 4)
-        store(4, 1, 0, 4)
-        first_step(4, 1, 4, 1, gram_g)
-        first_step(0, 4, 4, 1, gram_r)
-        for m in (2, 3):
-            second_step(m, 2, 2)
-            store(m, 1, 2, 2)
-        second_step_vector(4, 4, 1)
         for m in (0, 1):
-            second_step_vector(m, 4, 1)
+            second_step(m, 4, 1)
         store(0, 2, 4, 1)
-        second_step(2, 4, 1)
-        second_step_vector(3, 4, 1)
-        store(2, 3, 4, 1)
+        first_step(4, 1, 0, 4, gram_f)
+        first_step(4, 1, 4, 1, gram_g)
+        for m in (2, 3):
+            second_step(m, 4, 1)
+            second_step(m, 2, 2)
+            store(m, 1, 2, 3)
+        second_step_vector(4, 2, 3)
+        second_step(4, 0, 2)
+        store(4, 1, 0, 5)

@@ -95,12 +95,13 @@ def tile_rdm_module_s_kernel(tc, embeddings, out):
                 in_=grouped[:, t * P * PACK : (t + 1) * P * PACK],
             )
 
+        def spread_into(bank, b, t):
+            nc.tensor.transpose(bank[:, tile_cols(b)], sq_of(t).to_broadcast([P, P]), ident[:])
+
         def spread(first, count):
             bank = psum_sq.tile([P, count * P], F32, tag="sq%d" % first)
             for b in range(count):
-                nc.tensor.transpose(
-                    bank[:, tile_cols(b)], sq_of(first + b).to_broadcast([P, P]), ident[:]
-                )
+                spread_into(bank, b, first + b)
             return bank
 
         def keep_sq(first, count, bank):
@@ -174,10 +175,13 @@ def tile_rdm_module_s_kernel(tc, embeddings, out):
             square_sum(t)
         flip(0)
         flip(1)
-        keep_busy(1)
-        for t in range(2, TILES):
-            flip(t)
+        keep_busy(1, P // 2)
+        flip(2)
         sq_bank0 = spread(0, 2)
+        flip(3)
+        flip(4)
+        sq_bank2 = psum_sq.tile([P, 2 * P], F32, tag="sq2")
+        spread_into(sq_bank2, 0, 2)
         keep_busy(1, P // 2)
         regroup(0)
         regroup(1)
@@ -186,22 +190,24 @@ def tile_rdm_module_s_kernel(tc, embeddings, out):
         quantise(1)
         keep_sq(0, 2, sq_bank0)
         square_sum(4)
-        gram_a = gram(0, 2, 0, 2)
+        gram_a = [gram(m, 1, 0, 2) for m in range(2)]
         regroup(3)
         quantise(2)
         quantise(3)
-        first_step(0, 2, 0, 2, gram_a)
+        for m in range(2):
+            first_step(m, 1, 0, 2, gram_a[m])
         regroup(4, on_scalar=True)
         gram_b = gram(2, 2, 0, 2)
-        sq_bank2 = spread(2, 2)
+        spread_into(sq_bank2, 1, 3)
         sq_bank4 = spread(4, 1)
         second_step(0, 0, 2)
         store(0, 1, 0, 2)
         keep_sq(2, 2, sq_bank2)
         first_step(2, 2, 0, 2, gram_b)
         quantise(4)
-        second_step_vector(1, 0, 2)
+        second_step(1, 0, 2)
         store(1, 1, 0, 2)
+        keep_sq(4, 1, sq_bank4)
         gram_c = gram(0, 2, 2, 2)
         gram_r = gram(0, 4, 4, 1)
         gram_d = gram(2, 2, 2, 2)
@@ -211,7 +217,6 @@ def tile_rdm_module_s_kernel(tc, embeddings, out):
         for m in (2, 3):
             second_step(m, 0, 2)
             store(m, 1, 0, 2)
-        keep_sq(4, 1, sq_bank4)
         first_step(0, 4, 4, 1, gram_r)
         for m in (0, 1):
             second_step(m, 2, 2)

from contextlib import ExitStack

import concourse.mybir as mybir
from concourse.masks import make_identity

F32 = mybir.dt.float32
BF16 = mybir.dt.bfloat16
U32 = mybir.dt.uint32
U8 = mybir.dt.uint8
FP8X4 = mybir.dt.float8_e4m3fn_x4
ALU = mybir.AluOpType
ACT = mybir.ActivationFunctionType

P = 128
PACK = 4
ROWS = 640
FEATURES = 512
TILES = ROWS // P
HALVES = 2
LEFT = 512
LEFT_TILES = LEFT // P
RIGHT = ROWS - LEFT
PSUM_BANKS = 8

FLOPS = 2 * ROWS * ROWS * FEATURES


def tile_rdm_module_s_kernel(tc, embeddings, out):
    nc = tc.nc
    with ExitStack() as ctx:
        keep = ctx.enter_context(tc.tile_pool(name="keep", bufs=1))
        psum_sq = ctx.enter_context(tc.psum_pool(name="psum_sq", bufs=1))
        psum = ctx.enter_context(tc.psum_pool(name="psum", bufs=PSUM_BANKS - 3))
        ctx.enter_context(tc.manual_schedule())

        x = keep.tile([P, TILES, FEATURES], BF16)
        squares = keep.tile([P, TILES, FEATURES], BF16)
        sq_col_v = keep.tile([P, 1], F32)
        sq_col_s = keep.tile([P, TILES], F32)
        sq_row = keep.tile([P, ROWS], F32)
        ident = keep.tile([P, P], F32)
        grouped = keep.tile([P, ROWS * PACK], BF16, align_bytes=64)
        codes = keep.tile([P, ROWS], U32, align_bytes=64)
        scales = keep.tile([P, ROWS], U8, align_bytes=64)
        grouped_words = grouped[:].bitcast(F32).rearrange("p (i h) -> p i h", h=HALVES)
        partial = keep.tile([P, TILES, ROWS], F32)
        dist = keep.tile([P, TILES, ROWS], F32)
        out_tiles = out.rearrange("(m p) j -> p m j", p=P)

        def tile_cols(first, count=1):
            return slice(first * P, (first + count) * P)

        def square_sum(t):
            if t == 0:
                nc.vector.scalar_tensor_tensor(
                    out=squares[:, t, :],
                    in0=x[:, t, :],
                    scalar=1.0,
                    in1=x[:, t, :],
                    op0=ALU.mult,
                    op1=ALU.mult,
                    accum_out=sq_col_v[:],
                )
            else:
                nc.scalar.activation(
                    out=squares[:, t, :],
                    in_=x[:, t, :],
                    func=ACT.Square,
                    accum_out=sq_col_s[:, t : t + 1],
                )

        def sq_of(t):
            return sq_col_v[:] if t == 0 else sq_col_s[:, t : t + 1]

        flipped = {}

        def flip(t):
            words = x[:, t, :].bitcast(F32).rearrange("p (h w) -> p h w", h=HALVES)
            bank = psum.tile([P, HALVES, P], F32, tag="bank")
            for h in range(HALVES):
                nc.tensor.transpose(bank[:, h, :], words[:, h, :], ident[:])
            flipped[t] = bank

        def regroup(t, on_scalar=False):
            copy = nc.scalar.copy if on_scalar else nc.vector.tensor_copy
            copy(
                out=grouped_words[:, tile_cols(t), :],
                in_=flipped[t][:].rearrange("p h i -> p i h"),
            )

        def quantise(t):
            nc.vector.quantize_mx(
                out=codes[:, tile_cols(t)].bitcast(FP8X4),
                scales=scales[:, tile_cols(t)],
                in_=grouped[:, t * P * PACK : (t + 1) * P * PACK],
            )

        def spread_into(bank, b, t):
            nc.tensor.transpose(bank[:, tile_cols(b)], sq_of(t).to_broadcast([P, P]), ident[:])

        def spread(first, count):
            bank = psum_sq.tile([P, count * P], F32, tag="sq%d" % first)
            for b in range(count):
                spread_into(bank, b, first + b)
            return bank

        def keep_sq(first, count, bank):
            nc.scalar.copy(out=sq_row[:, tile_cols(first, count)], in_=bank[:])

        def gram(m, rows, c, cols):
            bank = psum.tile([P, rows, cols * P], F32, tag="bank")
            for b in range(rows):
                nc.tensor.matmul_mx(
                    out=bank[:, b, :],
                    lhsT=codes[:, tile_cols(m + b)].bitcast(FP8X4),
                    lhsT_scale=scales[:, tile_cols(m + b)],
                    rhs=codes[:, tile_cols(c, cols)].bitcast(FP8X4),
                    rhs_scale=scales[:, tile_cols(c, cols)],
                    start=True,
                    stop=True,
                )
            return bank

        def first_step(m, rows, c, cols, bank):
            nc.vector.scalar_tensor_tensor(
                out=partial[:, m : m + rows, tile_cols(c, cols)],
                in0=bank[:],
                scalar=-2.0,
                in1=sq_row[:, tile_cols(c, cols)].unsqueeze(1).to_broadcast([P, rows, cols * P]),
                op0=ALU.mult,
                op1=ALU.add,
            )

        def second_step(m, c, cols):
            nc.scalar.activation(
                out=dist[:, m, tile_cols(c, cols)],
                in_=partial[:, m, tile_cols(c, cols)],
                func=ACT.Relu,
                bias=sq_of(m),
                scale=1.0,
            )

        def second_step_vector(m, c, cols):
            nc.vector.tensor_scalar(
                out=dist[:, m, tile_cols(c, cols)],
                in0=partial[:, m, tile_cols(c, cols)],
                scalar1=sq_of(m),
                scalar2=0.0,
                op0=ALU.add,
                op1=ALU.max,
            )

        def store(m, rows, c, cols):
            nc.sync.dma_start(
                out=out_tiles[:, m : m + rows, tile_cols(c, cols)],
                in_=dist[:, m : m + rows, tile_cols(c, cols)],
            )

        for t in range(TILES):
            nc.sync.dma_start(out=x[:, t, :], in_=embeddings[tile_cols(t), :])
        zeros = keep.tile([P, P], F32)
        nc.vector.memset(zeros[:], 0.0)
        idle_bank = psum_sq.tile([P, P], F32, tag="sq4")

        def keep_busy(count, cols=P):
            for w in range(count):
                nc.tensor.matmul(
                    idle_bank[:, :cols], lhsT=zeros[:], rhs=zeros[:, :cols], start=True, stop=True
                )

        keep_busy(3)
        make_identity(nc, ident[:])

        for t in range(4):
            square_sum(t)
        flip(0)
        flip(1)
        keep_busy(1, P // 2)
        flip(2)
        sq_bank0 = spread(0, 2)
        flip(3)
        flip(4)
        sq_bank2 = psum_sq.tile([P, 2 * P], F32, tag="sq2")
        spread_into(sq_bank2, 0, 2)
        keep_busy(1, P // 2)
        regroup(0)
        regroup(1)
        quantise(0)
        regroup(2)
        quantise(1)
        keep_sq(0, 2, sq_bank0)
        square_sum(4)
        gram_a = [gram(m, 1, 0, 2) for m in range(2)]
        regroup(3)
        quantise(2)
        quantise(3)
        for m in range(2):
            first_step(m, 1, 0, 2, gram_a[m])
        regroup(4, on_scalar=True)
        gram_b = gram(2, 2, 0, 2)
        spread_into(sq_bank2, 1, 3)
        sq_bank4 = spread(4, 1)
        second_step(0, 0, 2)
        store(0, 1, 0, 2)
        keep_sq(2, 2, sq_bank2)
        first_step(2, 2, 0, 2, gram_b)
        quantise(4)
        second_step(1, 0, 2)
        store(1, 1, 0, 2)
        keep_sq(4, 1, sq_bank4)
        gram_c = gram(0, 2, 2, 2)
        gram_r = gram(0, 4, 4, 1)
        gram_d = gram(2, 2, 2, 2)
        gram_f = gram(4, 1, 0, 4)
        gram_g = gram(4, 1, 4, 1)
        first_step(0, 2, 2, 2, gram_c)
        for m in (2, 3):
            second_step(m, 0, 2)
            store(m, 1, 0, 2)
        first_step(0, 4, 4, 1, gram_r)
        for m in (0, 1):
            second_step(m, 2, 2)
            store(m, 1, 2, 2)
        first_step(2, 2, 2, 2, gram_d)
        for m in (0, 1):
            second_step(m, 4, 1)
        store(0, 2, 4, 1)
        first_step(4, 1, 0, 4, gram_f)
        first_step(4, 1, 4, 1, gram_g)
        for m in (2, 3):
            second_step(m, 4, 1)
            second_step(m, 2, 2)
            store(m, 1, 2, 3)
        second_step_vector(4, 2, 3)
        second_step(4, 0, 2)
        store(4, 1, 0, 5)
